import numpy as np
import ml_dtypes


def mxq(x, axis, fmt="e4m3"):
    dtype, down = {"e4m3": (ml_dtypes.float8_e4m3fn, 7), "e5m2": (ml_dtypes.float8_e5m2, 14)}[fmt]
    v = np.moveaxis(np.asarray(x, np.float32).astype(ml_dtypes.bfloat16).astype(np.float64), axis, -1)
    blocks = v.reshape(v.shape[:-1] + (-1, 32))
    amax = np.abs(blocks).max(-1, keepdims=True)
    byte = np.maximum(np.where(amax > 0, np.frexp(amax)[1] - 1 + 127, 0) - down, 1)
    scale = np.exp2(byte - 127.0)
    codes = (blocks / scale).astype(np.float32).astype(dtype).astype(np.float64)
    return np.moveaxis((codes * scale).reshape(v.shape), -1, axis)


WIDE = False


def mx_kscale(k):
    if not WIDE:
        return np.ones(k)
    levels = np.array([20, -20, 10, -10, 0])
    a = np.random.permutation(np.resize(levels, k // 512 * 4)).reshape(k // 512, 4)
    idx = np.arange(k)
    return np.exp2(a[idx // 512, idx % 128 // 32])


BF16 = ml_dtypes.bfloat16


def bf(x):
    return np.asarray(x, np.float32).astype(BF16)


def f64(x):
    return np.asarray(x).astype(np.float64)


B, S, D_IN, D_OUT = 2, 256, 2048, 2048
T = B * S


def quant8(w):
    mv = np.max(np.abs(w))
    q = np.ceil(np.log2(mv)) - 6.0
    scale = np.exp2(q)
    return np.round(w / scale) * scale


def setup_inputs():
    s = mx_kscale(T).reshape(B, S, 1)
    x = np.random.standard_normal((B, S, D_IN)) * s
    weight = np.random.standard_normal((D_OUT, D_IN)) * 3.0 / np.sqrt(D_IN)
    w_upper = quant8(weight)
    w_lower = weight - w_upper
    g = np.random.standard_normal((B, S, D_OUT)) * np.exp2(np.random.randint(-12, 1, (B, S, 1))) / s
    return {"x": bf(x), "weight_upper": bf(w_upper), "weight_lower": bf(w_lower), "grad_out": bf(g)}


def reference(x, weight_upper, weight_lower, grad_out):
    xt = f64(x).reshape(T, D_IN)
    gt = f64(grad_out).reshape(T, D_OUT)
    return mxq(gt, 0, "e5m2").T @ mxq(xt, 0, "e4m3")

@@ -1,0 +1,159 @@
+from contextlib import ExitStack
+
+import concourse.mybir as mybir
+
+P = 128
+PACK = 4
+TOKENS = P * PACK
+D_IN = 2048
+D_OUT = 2048
+N_TILE = 512
+ROWS = 4
+
+FLOPS = 2 * TOKENS * D_IN * D_OUT
+BYTES = 2 * TOKENS * (D_IN + D_OUT) + 4 * D_IN * D_OUT
+
+BF16 = mybir.dt.bfloat16
+F32 = mybir.dt.float32
+U32 = mybir.dt.uint32
+U8 = mybir.dt.uint8
+E4M3X4 = mybir.dt.float8_e4m3fn_x4
+E5M2X4 = mybir.dt.float8_e5m2_x4
+
+
+def tile_virtual16bmatmul_kernel(tc, x, weight_upper, weight_lower, grad_out, out):
+    nc = tc.nc
+    x_rows = x.flatten_outer_dims().rearrange("(p j) d -> p j d", j=PACK)
+    g_rows = grad_out.flatten_outer_dims().rearrange("(p j) d -> p j d", j=PACK)
+    out_rows = out.rearrange("(c q t) n -> c q t n", q=P, t=ROWS)
+
+    with ExitStack() as ctx:
+        keep = ctx.enter_context(tc.tile_pool(name="keep", bufs=1))
+        psum = ctx.enter_context(tc.psum_pool(name="psum", bufs=8))
+        ctx.enter_context(tc.manual_schedule())
+
+        x_raw = [keep.tile([P, PACK, 1024], BF16, name="x_raw%d" % i) for i in range(2)]
+        g_raw_first = keep.tile([P, PACK, 512], BF16, name="g_raw_first")
+        g_raw_rest = keep.tile([P, PACK, 1536], BF16, name="g_raw_rest")
+        nc.sync.dma_start(out=x_raw[0][:], in_=x_rows[:, :, 0:1024])
+        nc.sync.dma_start(out=g_raw_first[:], in_=g_rows[:, :, 0:512])
+        nc.sync.dma_start(out=x_raw[1][:], in_=x_rows[:, :, 1024:2048])
+        nc.sync.dma_start(out=g_raw_rest[:], in_=g_rows[:, :, 512:2048])
+
+        x_grouped = [
+            keep.tile([P, N_TILE, PACK], BF16, name="x_grouped%d" % u, align_bytes=64)
+            for u in range(4)
+        ]
+        x_codes = [keep.tile([P, N_TILE], U32, name="x_codes%d" % u, align_bytes=64) for u in range(4)]
+        x_scales = [keep.tile([P, N_TILE], U8, name="x_scales%d" % u, align_bytes=64) for u in range(4)]
+        g_grouped = [
+            keep.tile([P, 2, P, PACK], BF16, name="g_grouped%d" % k, align_bytes=64)
+            for k in range(8)
+        ]
+        g_codes = [keep.tile([P, 2, P], U32, name="g_codes%d" % k, align_bytes=64) for k in range(8)]
+        g_scales = [keep.tile([P, 2, P], U8, name="g_scales%d" % k, align_bytes=64) for k in range(8)]
+
+        vcopy = nc.vector.tensor_copy
+        scopy = nc.scalar.copy
+
+        def regroup_x(copy, u):
+            src = x_raw[u // 2][:, :, (u % 2) * N_TILE : (u % 2 + 1) * N_TILE]
+            copy(
+                out=x_grouped[u][:].rearrange("p (c i) j -> p c j i", i=4),
+                in_=src.rearrange("p j (c i) -> p c j i", i=4),
+            )
+
+        def quantise_x(u):
+            nc.vector.quantize_mx(
+                out=x_codes[u][:].bitcast(E4M3X4),
+                scales=x_scales[u][:],
+                in_=x_grouped[u][:].rearrange("p w j -> p (w j)"),
+            )
+
+        def regroup_g(k):
+            c, h = k // 2, k % 2
+            if c == 0:
+                src = g_raw_first[:, :, :]
+            else:
+                src = g_raw_rest[:, :, (c - 1) * 512 : c * 512]
+            vcopy(
+                out=g_grouped[k][:],
+                in_=src.rearrange("p j (q t) -> p t q j", t=ROWS)[:, 2 * h : 2 * h + 2, :, :],
+            )
+
+        def quantise_g(k):
+            nc.vector.quantize_mx(
+                out=g_codes[k][:].rearrange("p t q -> p (t q)").bitcast(E5M2X4),
+                scales=g_scales[k][:].rearrange("p t q -> p (t q)"),
+                in_=g_grouped[k][:].rearrange("p t q j -> p (t q j)"),
+            )
+
+        def one_pass(k, t, u):
+            acc = psum.tile([P, N_TILE], F32)
+            nc.tensor.matmul_mx(
+                out=acc[:],
+                lhsT=g_codes[k][:, t, :].bitcast(E5M2X4),
+                lhsT_scale=g_scales[k][:, t, :],
+                rhs=x_codes[u][:].bitcast(E4M3X4),
+                rhs_scale=x_scales[u][:],
+                start=True,
+                stop=True,
+            )
+            return acc
+
+        def drain(copy, stage, t, slot, acc):
+            copy(out=stage[:, t, slot * N_TILE : (slot + 1) * N_TILE], in_=acc[:])
+
+        stage = [keep.tile([P, 2, 1024], F32, name="stage_head%d" % i) for i in range(4)]
+
+        regroup_x(vcopy, 0)
+        regroup_x(scopy, 1)
+        regroup_g(0)
+        quantise_x(0)
+        quantise_g(0)
+        a00 = one_pass(0, 0, 0)
+        a10 = one_pass(0, 1, 0)
+        quantise_x(1)
+        a01 = one_pass(0, 0, 1)
+        a11 = one_pass(0, 1, 1)
+        regroup_g(1)
+        drain(scopy, stage[0], 0, 0, a00)
+        drain(scopy, stage[0], 1, 0, a10)
+        drain(scopy, stage[0], 0, 1, a01)
+        drain(vcopy, stage[0], 1, 1, a11)
+        nc.sync.dma_start(out=out_rows[0, :, 0:2, 0:1024], in_=stage[0][:])
+        quantise_g(1)
+
+        banks = [(t, s, one_pass(1, t, s)) for t in range(2) for s in range(2)]
+        regroup_x(vcopy, 2)
+        regroup_x(vcopy, 3)
+        for t, s, acc in banks:
+            drain(scopy, stage[1], t, s, acc)
+        nc.sync.dma_start(out=out_rows[0, :, 2:4, 0:1024], in_=stage[1][:])
+        quantise_x(2)
+        quantise_x(3)
+
+        banks = [(t, s, one_pass(0, t, 2 + s)) for t in range(2) for s in range(2)]
+        regroup_g(2)
+        for i, (t, s, acc) in enumerate(banks):
+            drain(vcopy if i % 2 == 1 else scopy, stage[2], t, s, acc)
+        nc.sync.dma_start(out=out_rows[0, :, 0:2, 1024:2048], in_=stage[2][:])
+
+        banks = [(t, s, one_pass(1, t, 2 + s)) for t in range(2) for s in range(2)]
+        for i, (t, s, acc) in enumerate(banks):
+            drain(vcopy if i % 2 == 1 else scopy, stage[3], t, s, acc)
+            if i == 1:
+                quantise_g(2)
+        nc.sync.dma_start(out=out_rows[0, :, 2:4, 1024:2048], in_=stage[3][:])
+
+        for k in range(2, 8):
+            c, h = k // 2, k % 2
+            wide = keep.tile([P, 2, D_IN], F32, name="stage%d" % k)
+            banks = [(t, s, one_pass(k, t, s)) for t in range(2) for s in range(4)]
+            if k + 1 < 8:
+                regroup_g(k + 1)
+            for i, (t, s, acc) in enumerate(banks):
+                drain(vcopy if i in (1, 4, 7) else scopy, wide, t, s, acc)
+                if i == 1 and k + 1 < 8:
+                    quantise_g(k + 1)
+            nc.sync.dma_start(out=out_rows[c, :, 2 * h : 2 * h + 2, :], in_=wide[:])

@@ -32,13 +32,17 @@ def tile_virtual16bmatmul_kernel(tc, x, weight_upper, weight_lower, grad_out, ou
         psum = ctx.enter_context(tc.psum_pool(name="psum", bufs=8))
         ctx.enter_context(tc.manual_schedule())
 
-        x_raw = [keep.tile([P, PACK, 1024], BF16, name="x_raw%d" % i) for i in range(2)]
+        x_raw_a = keep.tile([P, PACK, 512], BF16, name="x_raw_a")
         g_raw_first = keep.tile([P, PACK, 512], BF16, name="g_raw_first")
+        x_raw_b = keep.tile([P, PACK, 512], BF16, name="x_raw_b")
+        x_raw_cd = keep.tile([P, PACK, 1024], BF16, name="x_raw_cd")
         g_raw_rest = keep.tile([P, PACK, 1536], BF16, name="g_raw_rest")
-        nc.sync.dma_start(out=x_raw[0][:], in_=x_rows[:, :, 0:1024])
+        nc.sync.dma_start(out=x_raw_a[:], in_=x_rows[:, :, 0:512])
         nc.sync.dma_start(out=g_raw_first[:], in_=g_rows[:, :, 0:512])
-        nc.sync.dma_start(out=x_raw[1][:], in_=x_rows[:, :, 1024:2048])
+        nc.sync.dma_start(out=x_raw_b[:], in_=x_rows[:, :, 512:1024])
+        nc.sync.dma_start(out=x_raw_cd[:], in_=x_rows[:, :, 1024:2048])
         nc.sync.dma_start(out=g_raw_rest[:], in_=g_rows[:, :, 512:2048])
+        x_raw = [x_raw_a[:, :, :], x_raw_b[:, :, :], x_raw_cd[:, :, 0:512], x_raw_cd[:, :, 512:1024]]
 
         x_grouped = [
             keep.tile([P, N_TILE, PACK], BF16, name="x_grouped%d" % u, align_bytes=64)
@@ -46,21 +50,25 @@ def tile_virtual16bmatmul_kernel(tc, x, weight_upper, weight_lower, grad_out, ou
         ]
         x_codes = [keep.tile([P, N_TILE], U32, name="x_codes%d" % u, align_bytes=64) for u in range(4)]
         x_scales = [keep.tile([P, N_TILE], U8, name="x_scales%d" % u, align_bytes=64) for u in range(4)]
+        g_width = [1, 1, 1, 1, 2, 2, 2, 2, 2, 2]
         g_grouped = [
-            keep.tile([P, 2, P, PACK], BF16, name="g_grouped%d" % k, align_bytes=64)
-            for k in range(8)
+            keep.tile([P, w, P, PACK], BF16, name="g_grouped%d" % i, align_bytes=64)
+            for i, w in enumerate(g_width)
         ]
-        g_codes = [keep.tile([P, 2, P], U32, name="g_codes%d" % k, align_bytes=64) for k in range(8)]
-        g_scales = [keep.tile([P, 2, P], U8, name="g_scales%d" % k, align_bytes=64) for k in range(8)]
+        g_codes = [
+            keep.tile([P, w, P], U32, name="g_codes%d" % i, align_bytes=64) for i, w in enumerate(g_width)
+        ]
+        g_scales = [
+            keep.tile([P, w, P], U8, name="g_scales%d" % i, align_bytes=64) for i, w in enumerate(g_width)
+        ]
 
         vcopy = nc.vector.tensor_copy
         scopy = nc.scalar.copy
 
-        def regroup_x(copy, u):
-            src = x_raw[u // 2][:, :, (u % 2) * N_TILE : (u % 2 + 1) * N_TILE]
+        def regroup_x(copy, u, lo, hi):
             copy(
-                out=x_grouped[u][:].rearrange("p (c i) j -> p c j i", i=4),
-                in_=src.rearrange("p j (c i) -> p c j i", i=4),
+                out=x_grouped[u][:, lo:hi, :].rearrange("p (c i) j -> p c j i", i=4),
+                in_=x_raw[u][:, :, lo:hi].rearrange("p j (c i) -> p c j i", i=4),
             )
 
         def quantise_x(u):
@@ -70,30 +78,30 @@ def tile_virtual16bmatmul_kernel(tc, x, weight_upper, weight_lower, grad_out, ou
                 in_=x_grouped[u][:].rearrange("p w j -> p (w j)"),
             )
 
-        def regroup_g(k):
-            c, h = k // 2, k % 2
-            if c == 0:
-                src = g_raw_first[:, :, :]
+        def regroup_g(copy, i):
+            if i < 4:
+                src, t0 = g_raw_first[:, :, :], i
             else:
-                src = g_raw_rest[:, :, (c - 1) * 512 : c * 512]
-            vcopy(
-                out=g_grouped[k][:],
-                in_=src.rearrange("p j (q t) -> p t q j", t=ROWS)[:, 2 * h : 2 * h + 2, :, :],
+                c = (i - 4) // 2
+                src, t0 = g_raw_rest[:, :, c * 512 : (c + 1) * 512], 2 * ((i - 4) % 2)
+            copy(
+                out=g_grouped[i][:],
+                in_=src.rearrange("p j (q t) -> p t q j", t=ROWS)[:, t0 : t0 + g_width[i], :, :],
             )
 
-        def quantise_g(k):
+        def quantise_g(i):
             nc.vector.quantize_mx(
-                out=g_codes[k][:].rearrange("p t q -> p (t q)").bitcast(E5M2X4),
-                scales=g_scales[k][:].rearrange("p t q -> p (t q)"),
-                in_=g_grouped[k][:].rearrange("p t q j -> p (t q j)"),
+                out=g_codes[i][:].rearrange("p t q -> p (t q)").bitcast(E5M2X4),
+                scales=g_scales[i][:].rearrange("p t q -> p (t q)"),
+                in_=g_grouped[i][:].rearrange("p t q j -> p (t q j)"),
             )
 
-        def one_pass(k, t, u):
+        def one_pass(i, t, u):
             acc = psum.tile([P, N_TILE], F32)
             nc.tensor.matmul_mx(
                 out=acc[:],
-                lhsT=g_codes[k][:, t, :].bitcast(E5M2X4),
-                lhsT_scale=g_scales[k][:, t, :],
+                lhsT=g_codes[i][:, t, :].bitcast(E5M2X4),
+                lhsT_scale=g_scales[i][:, t, :],
                 rhs=x_codes[u][:].bitcast(E4M3X4),
                 rhs_scale=x_scales[u][:],
                 start=True,
@@ -101,59 +109,56 @@ def tile_virtual16bmatmul_kernel(tc, x, weight_upper, weight_lower, grad_out, ou
             )
             return acc
 
-        def drain(copy, stage, t, slot, acc):
-            copy(out=stage[:, t, slot * N_TILE : (slot + 1) * N_TILE], in_=acc[:])
-
-        stage = [keep.tile([P, 2, 1024], F32, name="stage_head%d" % i) for i in range(4)]
-
-        regroup_x(vcopy, 0)
-        regroup_x(scopy, 1)
-        regroup_g(0)
+        regroup_x(vcopy, 0, 0, 320)
+        regroup_x(scopy, 0, 320, 512)
         quantise_x(0)
+        regroup_g(vcopy, 0)
+        regroup_g(scopy, 1)
+        regroup_g(scopy, 2)
+        regroup_g(scopy, 3)
         quantise_g(0)
-        a00 = one_pass(0, 0, 0)
-        a10 = one_pass(0, 1, 0)
-        quantise_x(1)
-        a01 = one_pass(0, 0, 1)
-        a11 = one_pass(0, 1, 1)
-        regroup_g(1)
-        drain(scopy, stage[0], 0, 0, a00)
-        drain(scopy, stage[0], 1, 0, a10)
-        drain(scopy, stage[0], 0, 1, a01)
-        drain(vcopy, stage[0], 1, 1, a11)
-        nc.sync.dma_start(out=out_rows[0, :, 0:2, 0:1024], in_=stage[0][:])
+        acc_a = [one_pass(0, 0, 0)]
         quantise_g(1)
-
-        banks = [(t, s, one_pass(1, t, s)) for t in range(2) for s in range(2)]
-        regroup_x(vcopy, 2)
-        regroup_x(vcopy, 3)
-        for t, s, acc in banks:
-            drain(scopy, stage[1], t, s, acc)
-        nc.sync.dma_start(out=out_rows[0, :, 2:4, 0:1024], in_=stage[1][:])
+        acc_a.append(one_pass(1, 0, 0))
+        regroup_x(vcopy, 1, 0, 256)
+        quantise_g(2)
+        acc_a.append(one_pass(2, 0, 0))
+        regroup_x(vcopy, 1, 256, 512)
+        quantise_g(3)
+        acc_a.append(one_pass(3, 0, 0))
+        for t in range(4):
+            small = keep.tile([P, N_TILE], F32, name="stage_a%d" % t)
+            scopy(out=small[:], in_=acc_a[t][:])
+            nc.sync.dma_start(out=out_rows[0, :, t, 0:512], in_=small[:])
+        quantise_x(1)
+        acc_b = [one_pass(t, 0, 1) for t in range(4)]
+        regroup_x(vcopy, 2, 0, 512)
+        regroup_x(vcopy, 3, 0, 512)
+        for t in range(4):
+            small = keep.tile([P, N_TILE], F32, name="stage_b%d" % t)
+            scopy(out=small[:], in_=acc_b[t][:])
+            nc.sync.dma_start(out=out_rows[0, :, t, 512:1024], in_=small[:])
         quantise_x(2)
         quantise_x(3)
+        acc_cd = [(one_pass(t, 0, 2), one_pass(t, 0, 3)) for t in range(4)]
+        regroup_g(vcopy, 4)
+        for t in range(4):
+            half = keep.tile([P, 2 * N_TILE], F32, name="stage_cd%d" % t)
+            scopy(out=half[:, 0:512], in_=acc_cd[t][0][:])
+            vcopy(out=half[:, 512:1024], in_=acc_cd[t][1][:])
+            nc.sync.dma_start(out=out_rows[0, :, t, 1024:2048], in_=half[:])
+            if t == 0:
+                quantise_g(4)
 
-        banks = [(t, s, one_pass(0, t, 2 + s)) for t in range(2) for s in range(2)]
-        regroup_g(2)
-        for i, (t, s, acc) in enumerate(banks):
-            drain(vcopy if i % 2 == 1 else scopy, stage[2], t, s, acc)
-        nc.sync.dma_start(out=out_rows[0, :, 0:2, 1024:2048], in_=stage[2][:])
-
-        banks = [(t, s, one_pass(1, t, 2 + s)) for t in range(2) for s in range(2)]
-        for i, (t, s, acc) in enumerate(banks):
-            drain(vcopy if i % 2 == 1 else scopy, stage[3], t, s, acc)
-            if i == 1:
-                quantise_g(2)
-        nc.sync.dma_start(out=out_rows[0, :, 2:4, 1024:2048], in_=stage[3][:])
-
-        for k in range(2, 8):
-            c, h = k // 2, k % 2
-            wide = keep.tile([P, 2, D_IN], F32, name="stage%d" % k)
-            banks = [(t, s, one_pass(k, t, s)) for t in range(2) for s in range(4)]
-            if k + 1 < 8:
-                regroup_g(k + 1)
-            for i, (t, s, acc) in enumerate(banks):
-                drain(vcopy if i in (1, 4, 7) else scopy, wide, t, s, acc)
-                if i == 1 and k + 1 < 8:
-                    quantise_g(k + 1)
+        for i in range(4, 10):
+            c, h = 1 + (i - 4) // 2, (i - 4) % 2
+            wide = keep.tile([P, 2, D_IN], F32, name="stage%d" % i)
+            banks = [(t, s, one_pass(i, t, s)) for t in range(2) for s in range(4)]
+            if i + 1 < 10:
+                regroup_g(vcopy, i + 1)
+            for n, (t, s, acc) in enumerate(banks):
+                copy = vcopy if n in (1, 4, 7) else scopy
+                copy(out=wide[:, t, s * N_TILE : (s + 1) * N_TILE], in_=acc[:])
+                if n == 1 and i + 1 < 10:
+                    quantise_g(i + 1)
             nc.sync.dma_start(out=out_rows[c, :, 2 * h : 2 * h + 2, :], in_=wide[:])

@@ -133,7 +133,8 @@ def tile_virtual16bmatmul_kernel(tc, x, weight_upper, weight_lower, grad_out, ou
         quantise_x(1)
         acc_b = [one_pass(t, 0, 1) for t in range(4)]
         regroup_x(vcopy, 2, 0, 512)
-        regroup_x(vcopy, 3, 0, 512)
+        regroup_x(scopy, 3, 320, 512)
+        regroup_x(vcopy, 3, 0, 320)
         for t in range(4):
             small = keep.tile([P, N_TILE], F32, name="stage_b%d" % t)
             scopy(out=small[:], in_=acc_b[t][:])
@@ -152,13 +153,29 @@ def tile_virtual16bmatmul_kernel(tc, x, weight_upper, weight_lower, grad_out, ou
 
         for i in range(4, 10):
             c, h = 1 + (i - 4) // 2, (i - 4) % 2
-            wide = keep.tile([P, 2, D_IN], F32, name="stage%d" % i)
             banks = [(t, s, one_pass(i, t, s)) for t in range(2) for s in range(4)]
             if i + 1 < 10:
                 regroup_g(vcopy, i + 1)
             for n, (t, s, acc) in enumerate(banks):
+                if i == 4:
+                    if s == 0:
+                        wide = keep.tile([P, 1, D_IN], F32, name="stage4_%d" % t)
+                    row = 0
+                elif i == 5:
+                    if n == 0:
+                        wide = keep.tile([P, 2, D_IN], F32, name="stage5")
+                    row = t
+                else:
+                    if n == 0 and h == 0:
+                        wide = keep.tile([P, 4, D_IN], F32, name="stage_block%d" % c)
+                    row = 2 * h + t
                 copy = vcopy if n in (1, 4, 7) else scopy
-                copy(out=wide[:, t, s * N_TILE : (s + 1) * N_TILE], in_=acc[:])
+                copy(out=wide[:, row, s * N_TILE : (s + 1) * N_TILE], in_=acc[:])
                 if n == 1 and i + 1 < 10:
                     quantise_g(i + 1)
-            nc.sync.dma_start(out=out_rows[c, :, 2 * h : 2 * h + 2, :], in_=wide[:])
+                if i == 4 and s == 3:
+                    nc.sync.dma_start(out=out_rows[c, :, t : t + 1, :], in_=wide[:])
+            if i == 5:
+                nc.sync.dma_start(out=out_rows[c, :, 2:4, :], in_=wide[:])
+            if i > 5 and h == 1:
+                nc.sync.dma_start(out=out_rows[c, :, :, :], in_=wide[:])

@@ -9,6 +9,7 @@ D_IN = 2048
 D_OUT = 2048
 N_TILE = 512
 ROWS = 4
+DMA_ALIGN = 1024
 
 FLOPS = 2 * TOKENS * D_IN * D_OUT
 BYTES = 2 * TOKENS * (D_IN + D_OUT) + 4 * D_IN * D_OUT
@@ -32,11 +33,11 @@ def tile_virtual16bmatmul_kernel(tc, x, weight_upper, weight_lower, grad_out, ou
         psum = ctx.enter_context(tc.psum_pool(name="psum", bufs=8))
         ctx.enter_context(tc.manual_schedule())
 
-        x_raw_a = keep.tile([P, PACK, 512], BF16, name="x_raw_a")
-        g_raw_first = keep.tile([P, PACK, 512], BF16, name="g_raw_first")
-        x_raw_b = keep.tile([P, PACK, 512], BF16, name="x_raw_b")
-        x_raw_cd = keep.tile([P, PACK, 1024], BF16, name="x_raw_cd")
-        g_raw_rest = keep.tile([P, PACK, 1536], BF16, name="g_raw_rest")
+        x_raw_a = keep.tile([P, PACK, 512], BF16, name="x_raw_a", align_bytes=DMA_ALIGN)
+        g_raw_first = keep.tile([P, PACK, 512], BF16, name="g_raw_first", align_bytes=DMA_ALIGN)
+        x_raw_b = keep.tile([P, PACK, 512], BF16, name="x_raw_b", align_bytes=DMA_ALIGN)
+        x_raw_cd = keep.tile([P, PACK, 1024], BF16, name="x_raw_cd", align_bytes=DMA_ALIGN)
+        g_raw_rest = keep.tile([P, PACK, 1536], BF16, name="g_raw_rest", align_bytes=DMA_ALIGN)
         nc.sync.dma_start(out=x_raw_a[:], in_=x_rows[:, :, 0:512])
         nc.sync.dma_start(out=g_raw_first[:], in_=g_rows[:, :, 0:512])
         nc.sync.dma_start(out=x_raw_b[:], in_=x_rows[:, :, 512:1024])
@@ -127,7 +128,7 @@ def tile_virtual16bmatmul_kernel(tc, x, weight_upper, weight_lower, grad_out, ou
         quantise_g(3)
         acc_a.append(one_pass(3, 0, 0))
         for t in range(4):
-            small = keep.tile([P, N_TILE], F32, name="stage_a%d" % t)
+            small = keep.tile([P, N_TILE], F32, name="stage_a%d" % t, align_bytes=DMA_ALIGN)
             scopy(out=small[:], in_=acc_a[t][:])
             nc.sync.dma_start(out=out_rows[0, :, t, 0:512], in_=small[:])
         quantise_x(1)
@@ -136,7 +137,7 @@ def tile_virtual16bmatmul_kernel(tc, x, weight_upper, weight_lower, grad_out, ou
         regroup_x(scopy, 3, 320, 512)
         regroup_x(vcopy, 3, 0, 320)
         for t in range(4):
-            small = keep.tile([P, N_TILE], F32, name="stage_b%d" % t)
+            small = keep.tile([P, N_TILE], F32, name="stage_b%d" % t, align_bytes=DMA_ALIGN)
             scopy(out=small[:], in_=acc_b[t][:])
             nc.sync.dma_start(out=out_rows[0, :, t, 512:1024], in_=small[:])
         quantise_x(2)
@@ -144,7 +145,7 @@ def tile_virtual16bmatmul_kernel(tc, x, weight_upper, weight_lower, grad_out, ou
         acc_cd = [(one_pass(t, 0, 2), one_pass(t, 0, 3)) for t in range(4)]
         regroup_g(vcopy, 4)
         for t in range(4):
-            half = keep.tile([P, 2 * N_TILE], F32, name="stage_cd%d" % t)
+            half = keep.tile([P, 2 * N_TILE], F32, name="stage_cd%d" % t, align_bytes=DMA_ALIGN)
             scopy(out=half[:, 0:512], in_=acc_cd[t][0][:])
             vcopy(out=half[:, 512:1024], in_=acc_cd[t][1][:])
             nc.sync.dma_start(out=out_rows[0, :, t, 1024:2048], in_=half[:])
@@ -159,15 +160,15 @@ def tile_virtual16bmatmul_kernel(tc, x, weight_upper, weight_lower, grad_out, ou
             for n, (t, s, acc) in enumerate(banks):
                 if i == 4:
                     if s == 0:
-                        wide = keep.tile([P, 1, D_IN], F32, name="stage4_%d" % t)
+                        wide = keep.tile([P, 1, D_IN], F32, name="stage4_%d" % t, align_bytes=DMA_ALIGN)
                     row = 0
                 elif i == 5:
                     if n == 0:
-                        wide = keep.tile([P, 2, D_IN], F32, name="stage5")
+                        wide = keep.tile([P, 2, D_IN], F32, name="stage5", align_bytes=DMA_ALIGN)
                     row = t
                 else:
                     if n == 0 and h == 0:
-                        wide = keep.tile([P, 4, D_IN], F32, name="stage_block%d" % c)
+                        wide = keep.tile([P, 4, D_IN], F32, name="stage_block%d" % c, align_bytes=DMA_ALIGN)
                     row = 2 * h + t
                 copy = vcopy if n in (1, 4, 7) else scopy
                 copy(out=wide[:, row, s * N_TILE : (s + 1) * N_TILE], in_=acc[:])

@@ -33,17 +33,19 @@ def tile_virtual16bmatmul_kernel(tc, x, weight_upper, weight_lower, grad_out, ou
         psum = ctx.enter_context(tc.psum_pool(name="psum", bufs=8))
         ctx.enter_context(tc.manual_schedule())
 
-        x_raw_a = keep.tile([P, PACK, 512], BF16, name="x_raw_a", align_bytes=DMA_ALIGN)
+        x_raw_a0 = keep.tile([P, PACK, 256], BF16, name="x_raw_a0", align_bytes=DMA_ALIGN)
+        x_raw_a1 = keep.tile([P, PACK, 256], BF16, name="x_raw_a1", align_bytes=DMA_ALIGN)
         g_raw_first = keep.tile([P, PACK, 512], BF16, name="g_raw_first", align_bytes=DMA_ALIGN)
         x_raw_b = keep.tile([P, PACK, 512], BF16, name="x_raw_b", align_bytes=DMA_ALIGN)
         x_raw_cd = keep.tile([P, PACK, 1024], BF16, name="x_raw_cd", align_bytes=DMA_ALIGN)
         g_raw_rest = keep.tile([P, PACK, 1536], BF16, name="g_raw_rest", align_bytes=DMA_ALIGN)
-        nc.sync.dma_start(out=x_raw_a[:], in_=x_rows[:, :, 0:512])
+        nc.sync.dma_start(out=x_raw_a0[:], in_=x_rows[:, :, 0:256])
+        nc.sync.dma_start(out=x_raw_a1[:], in_=x_rows[:, :, 256:512])
         nc.sync.dma_start(out=g_raw_first[:], in_=g_rows[:, :, 0:512])
         nc.sync.dma_start(out=x_raw_b[:], in_=x_rows[:, :, 512:1024])
         nc.sync.dma_start(out=x_raw_cd[:], in_=x_rows[:, :, 1024:2048])
         nc.sync.dma_start(out=g_raw_rest[:], in_=g_rows[:, :, 512:2048])
-        x_raw = [x_raw_a[:, :, :], x_raw_b[:, :, :], x_raw_cd[:, :, 0:512], x_raw_cd[:, :, 512:1024]]
+        x_raw = [None, x_raw_b[:, :, :], x_raw_cd[:, :, 0:512], x_raw_cd[:, :, 512:1024]]
 
         x_grouped = [
             keep.tile([P, N_TILE, PACK], BF16, name="x_grouped%d" % u, align_bytes=64)
@@ -70,6 +72,12 @@ def tile_virtual16bmatmul_kernel(tc, x, weight_upper, weight_lower, grad_out, ou
             copy(
                 out=x_grouped[u][:, lo:hi, :].rearrange("p (c i) j -> p c j i", i=4),
                 in_=x_raw[u][:, :, lo:hi].rearrange("p j (c i) -> p c j i", i=4),
+            )
+
+        def regroup_first(copy, half, lo, hi):
+            copy(
+                out=x_grouped[0][:, 256 * half + lo : 256 * half + hi, :].rearrange("p (c i) j -> p c j i", i=4),
+                in_=(x_raw_a0, x_raw_a1)[half][:, :, lo:hi].rearrange("p j (c i) -> p c j i", i=4),
             )
 
         def quantise_x(u):
@@ -110,8 +118,9 @@ def tile_virtual16bmatmul_kernel(tc, x, weight_upper, weight_lower, grad_out, ou
             )
             return acc
 
-        regroup_x(vcopy, 0, 0, 320)
-        regroup_x(scopy, 0, 320, 512)
+        regroup_first(vcopy, 0, 0, 256)
+        regroup_first(vcopy, 1, 0, 192)
+        regroup_first(scopy, 1, 192, 256)
         quantise_x(0)
         regroup_g(vcopy, 0)
         regroup_g(scopy, 1)

@@ -125,7 +125,7 @@ def tile_virtual16bmatmul_kernel(tc, x, weight_upper, weight_lower, grad_out, ou
         regroup_g(vcopy, 0)
         regroup_g(scopy, 1)
         regroup_g(scopy, 2)
-        regroup_g(scopy, 3)
+        regroup_g(vcopy, 3)
         quantise_g(0)
         acc_a = [one_pass(0, 0, 0)]
         quantise_g(1)
@@ -136,28 +136,39 @@ def tile_virtual16bmatmul_kernel(tc, x, weight_upper, weight_lower, grad_out, ou
         regroup_x(vcopy, 1, 256, 512)
         quantise_g(3)
         acc_a.append(one_pass(3, 0, 0))
-        for t in range(4):
-            small = keep.tile([P, N_TILE], F32, name="stage_a%d" % t, align_bytes=DMA_ALIGN)
-            scopy(out=small[:], in_=acc_a[t][:])
-            nc.sync.dma_start(out=out_rows[0, :, t, 0:512], in_=small[:])
+        for h in range(2):
+            pair = keep.tile([P, 2, N_TILE], F32, name="stage_a%d" % h, align_bytes=DMA_ALIGN)
+            for i in range(2):
+                scopy(out=pair[:, i, :], in_=acc_a[2 * h + i][:])
+            nc.sync.dma_start(out=out_rows[0, :, 2 * h : 2 * h + 2, 0:512], in_=pair[:])
         quantise_x(1)
         acc_b = [one_pass(t, 0, 1) for t in range(4)]
         regroup_x(vcopy, 2, 0, 512)
-        regroup_x(scopy, 3, 320, 512)
-        regroup_x(vcopy, 3, 0, 320)
-        for t in range(4):
-            small = keep.tile([P, N_TILE], F32, name="stage_b%d" % t, align_bytes=DMA_ALIGN)
-            scopy(out=small[:], in_=acc_b[t][:])
-            nc.sync.dma_start(out=out_rows[0, :, t, 512:1024], in_=small[:])
+        regroup_x(scopy, 3, 448, 512)
+        regroup_x(vcopy, 3, 0, 448)
+        for h in range(2):
+            pair = keep.tile([P, 2, N_TILE], F32, name="stage_b%d" % h, align_bytes=DMA_ALIGN)
+            for i in range(2):
+                scopy(out=pair[:, i, :], in_=acc_b[2 * h + i][:])
+            nc.sync.dma_start(out=out_rows[0, :, 2 * h : 2 * h + 2, 512:1024], in_=pair[:])
         quantise_x(2)
         quantise_x(3)
         acc_cd = [(one_pass(t, 0, 2), one_pass(t, 0, 3)) for t in range(4)]
         regroup_g(vcopy, 4)
+        last = keep.tile([P, 2, 2 * N_TILE], F32, name="stage_cd23", align_bytes=DMA_ALIGN)
         for t in range(4):
-            half = keep.tile([P, 2 * N_TILE], F32, name="stage_cd%d" % t, align_bytes=DMA_ALIGN)
-            scopy(out=half[:, 0:512], in_=acc_cd[t][0][:])
-            vcopy(out=half[:, 512:1024], in_=acc_cd[t][1][:])
-            nc.sync.dma_start(out=out_rows[0, :, t, 1024:2048], in_=half[:])
+            if t < 2:
+                half = keep.tile([P, 1, 2 * N_TILE], F32, name="stage_cd%d" % t, align_bytes=DMA_ALIGN)
+                row = 0
+            else:
+                half = last
+                row = t - 2
+            scopy(out=half[:, row, 0:512], in_=acc_cd[t][0][:])
+            vcopy(out=half[:, row, 512:1024], in_=acc_cd[t][1][:])
+            if t < 2:
+                nc.sync.dma_start(out=out_rows[0, :, t : t + 1, 1024:2048], in_=half[:])
+            if t == 3:
+                nc.sync.dma_start(out=out_rows[0, :, 2:4, 1024:2048], in_=half[:])
             if t == 0:
                 quantise_g(4)
 

@@ -65,6 +65,8 @@ def tile_virtual16bmatmul_kernel(tc, x, weight_upper, weight_lower, grad_out, ou
             keep.tile([P, w, P], U8, name="g_scales%d" % i, align_bytes=64) for i, w in enumerate(g_width)
         ]
 
+        stage = keep.tile([P, 4, ROWS, D_IN], F32, name="stage", align_bytes=DMA_ALIGN)
+
         vcopy = nc.vector.tensor_copy
         scopy = nc.scalar.copy
 
@@ -118,6 +120,9 @@ def tile_virtual16bmatmul_kernel(tc, x, weight_upper, weight_lower, grad_out, ou
             )
             return acc
 
+        def store(c, t0, t1, n0, n1):
+            nc.sync.dma_start(out=out_rows[c, :, t0:t1, n0:n1], in_=stage[:, c, t0:t1, n0:n1])
+
         regroup_first(vcopy, 0, 0, 256)
         regroup_first(vcopy, 1, 0, 192)
         regroup_first(scopy, 1, 192, 256)
@@ -136,39 +141,30 @@ def tile_virtual16bmatmul_kernel(tc, x, weight_upper, weight_lower, grad_out, ou
         regroup_x(vcopy, 1, 256, 512)
         quantise_g(3)
         acc_a.append(one_pass(3, 0, 0))
-        for h in range(2):
-            pair = keep.tile([P, 2, N_TILE], F32, name="stage_a%d" % h, align_bytes=DMA_ALIGN)
-            for i in range(2):
-                scopy(out=pair[:, i, :], in_=acc_a[2 * h + i][:])
-            nc.sync.dma_start(out=out_rows[0, :, 2 * h : 2 * h + 2, 0:512], in_=pair[:])
+        for t in range(4):
+            scopy(out=stage[:, 0, t, 0:512], in_=acc_a[t][:])
+            if t % 2 == 1:
+                store(0, t - 1, t + 1, 0, 512)
         quantise_x(1)
         acc_b = [one_pass(t, 0, 1) for t in range(4)]
         regroup_x(vcopy, 2, 0, 512)
         regroup_x(scopy, 3, 448, 512)
         regroup_x(vcopy, 3, 0, 448)
-        for h in range(2):
-            pair = keep.tile([P, 2, N_TILE], F32, name="stage_b%d" % h, align_bytes=DMA_ALIGN)
-            for i in range(2):
-                scopy(out=pair[:, i, :], in_=acc_b[2 * h + i][:])
-            nc.sync.dma_start(out=out_rows[0, :, 2 * h : 2 * h + 2, 512:1024], in_=pair[:])
+        for t in range(4):
+            scopy(out=stage[:, 0, t, 512:1024], in_=acc_b[t][:])
+            if t % 2 == 1:
+                store(0, t - 1, t + 1, 512, 1024)
         quantise_x(2)
         quantise_x(3)
         acc_cd = [(one_pass(t, 0, 2), one_pass(t, 0, 3)) for t in range(4)]
         regroup_g(vcopy, 4)
-        last = keep.tile([P, 2, 2 * N_TILE], F32, name="stage_cd23", align_bytes=DMA_ALIGN)
         for t in range(4):
+            scopy(out=stage[:, 0, t, 1024:1536], in_=acc_cd[t][0][:])
+            vcopy(out=stage[:, 0, t, 1536:2048], in_=acc_cd[t][1][:])
             if t < 2:
-                half = keep.tile([P, 1, 2 * N_TILE], F32, name="stage_cd%d" % t, align_bytes=DMA_ALIGN)
-                row = 0
-            else:
-                half = last
-                row = t - 2
-            scopy(out=half[:, row, 0:512], in_=acc_cd[t][0][:])
-            vcopy(out=half[:, row, 512:1024], in_=acc_cd[t][1][:])
-            if t < 2:
-                nc.sync.dma_start(out=out_rows[0, :, t : t + 1, 1024:2048], in_=half[:])
+                store(0, t, t + 1, 1024, 2048)
             if t == 3:
-                nc.sync.dma_start(out=out_rows[0, :, 2:4, 1024:2048], in_=half[:])
+                store(0, 2, 4, 1024, 2048)
             if t == 0:
                 quantise_g(4)
 
@@ -178,25 +174,13 @@ def tile_virtual16bmatmul_kernel(tc, x, weight_upper, weight_lower, grad_out, ou
             if i + 1 < 10:
                 regroup_g(vcopy, i + 1)
             for n, (t, s, acc) in enumerate(banks):
-                if i == 4:
-                    if s == 0:
-                        wide = keep.tile([P, 1, D_IN], F32, name="stage4_%d" % t, align_bytes=DMA_ALIGN)
-                    row = 0
-                elif i == 5:
-                    if n == 0:
-                        wide = keep.tile([P, 2, D_IN], F32, name="stage5", align_bytes=DMA_ALIGN)
-                    row = t
-                else:
-                    if n == 0 and h == 0:
-                        wide = keep.tile([P, 4, D_IN], F32, name="stage_block%d" % c, align_bytes=DMA_ALIGN)
-                    row = 2 * h + t
                 copy = vcopy if n in (1, 4, 7) else scopy
-                copy(out=wide[:, row, s * N_TILE : (s + 1) * N_TILE], in_=acc[:])
+                copy(out=stage[:, c, 2 * h + t, s * N_TILE : (s + 1) * N_TILE], in_=acc[:])
                 if n == 1 and i + 1 < 10:
                     quantise_g(i + 1)
                 if i == 4 and s == 3:
-                    nc.sync.dma_start(out=out_rows[c, :, t : t + 1, :], in_=wide[:])
+                    store(c, t, t + 1, 0, D_IN)
             if i == 5:
-                nc.sync.dma_start(out=out_rows[c, :, 2:4, :], in_=wide[:])
+                store(c, 2, 4, 0, D_IN)
             if i > 5 and h == 1:
-                nc.sync.dma_start(out=out_rows[c, :, :, :], in_=wide[:])
+                store(c, 0, 4, 0, D_IN)

@@ -156,7 +156,11 @@ def tile_virtual16bmatmul_kernel(tc, x, weight_upper, weight_lower, grad_out, ou
                 store(0, t - 1, t + 1, 512, 1024)
         quantise_x(2)
         quantise_x(3)
-        acc_cd = [(one_pass(t, 0, 2), one_pass(t, 0, 3)) for t in range(4)]
+        acc_c = [one_pass(0, 0, 2), one_pass(1, 0, 2)]
+        acc_d = [one_pass(0, 0, 3), one_pass(1, 0, 3)]
+        acc_c.extend([one_pass(2, 0, 2), one_pass(3, 0, 2)])
+        acc_d.extend([one_pass(2, 0, 3), one_pass(3, 0, 3)])
+        acc_cd = [(acc_c[t], acc_d[t]) for t in range(4)]
         regroup_g(vcopy, 4)
         for t in range(4):
             scopy(out=stage[:, 0, t, 1024:1536], in_=acc_cd[t][0][:])

from contextlib import ExitStack

import concourse.mybir as mybir

P = 128
PACK = 4
TOKENS = P * PACK
D_IN = 2048
D_OUT = 2048
N_TILE = 512
ROWS = 4
DMA_ALIGN = 1024

FLOPS = 2 * TOKENS * D_IN * D_OUT
BYTES = 2 * TOKENS * (D_IN + D_OUT) + 4 * D_IN * D_OUT

BF16 = mybir.dt.bfloat16
F32 = mybir.dt.float32
U32 = mybir.dt.uint32
U8 = mybir.dt.uint8
E4M3X4 = mybir.dt.float8_e4m3fn_x4
E5M2X4 = mybir.dt.float8_e5m2_x4


def tile_virtual16bmatmul_kernel(tc, x, weight_upper, weight_lower, grad_out, out):
    nc = tc.nc
    x_rows = x.flatten_outer_dims().rearrange("(p j) d -> p j d", j=PACK)
    g_rows = grad_out.flatten_outer_dims().rearrange("(p j) d -> p j d", j=PACK)
    out_rows = out.rearrange("(c q t) n -> c q t n", q=P, t=ROWS)

    with ExitStack() as ctx:
        keep = ctx.enter_context(tc.tile_pool(name="keep", bufs=1))
        psum = ctx.enter_context(tc.psum_pool(name="psum", bufs=8))
        ctx.enter_context(tc.manual_schedule())

        x_raw_a0 = keep.tile([P, PACK, 256], BF16, name="x_raw_a0", align_bytes=DMA_ALIGN)
        x_raw_a1 = keep.tile([P, PACK, 256], BF16, name="x_raw_a1", align_bytes=DMA_ALIGN)
        g_raw_first = keep.tile([P, PACK, 512], BF16, name="g_raw_first", align_bytes=DMA_ALIGN)
        x_raw_b = keep.tile([P, PACK, 512], BF16, name="x_raw_b", align_bytes=DMA_ALIGN)
        x_raw_cd = keep.tile([P, PACK, 1024], BF16, name="x_raw_cd", align_bytes=DMA_ALIGN)
        g_raw_rest = keep.tile([P, PACK, 1536], BF16, name="g_raw_rest", align_bytes=DMA_ALIGN)
        nc.sync.dma_start(out=x_raw_a0[:], in_=x_rows[:, :, 0:256])
        nc.sync.dma_start(out=x_raw_a1[:], in_=x_rows[:, :, 256:512])
        nc.sync.dma_start(out=g_raw_first[:], in_=g_rows[:, :, 0:512])
        nc.sync.dma_start(out=x_raw_b[:], in_=x_rows[:, :, 512:1024])
        nc.sync.dma_start(out=x_raw_cd[:], in_=x_rows[:, :, 1024:2048])
        nc.sync.dma_start(out=g_raw_rest[:], in_=g_rows[:, :, 512:2048])
        x_raw = [None, x_raw_b[:, :, :], x_raw_cd[:, :, 0:512], x_raw_cd[:, :, 512:1024]]

        x_grouped = [
            keep.tile([P, N_TILE, PACK], BF16, name="x_grouped%d" % u, align_bytes=64)
            for u in range(4)
        ]
        x_codes = [keep.tile([P, N_TILE], U32, name="x_codes%d" % u, align_bytes=64) for u in range(4)]
        x_scales = [keep.tile([P, N_TILE], U8, name="x_scales%d" % u, align_bytes=64) for u in range(4)]
        g_width = [1, 1, 1, 1, 2, 2, 2, 2, 2, 2]
        g_grouped = [
            keep.tile([P, w, P, PACK], BF16, name="g_grouped%d" % i, align_bytes=64)
            for i, w in enumerate(g_width)
        ]
        g_codes = [
            keep.tile([P, w, P], U32, name="g_codes%d" % i, align_bytes=64) for i, w in enumerate(g_width)
        ]
        g_scales = [
            keep.tile([P, w, P], U8, name="g_scales%d" % i, align_bytes=64) for i, w in enumerate(g_width)
        ]

        stage = keep.tile([P, 4, ROWS, D_IN], F32, name="stage", align_bytes=DMA_ALIGN)

        vcopy = nc.vector.tensor_copy
        scopy = nc.scalar.copy

        def regroup_x(copy, u, lo, hi):
            copy(
                out=x_grouped[u][:, lo:hi, :].rearrange("p (c i) j -> p c j i", i=4),
                in_=x_raw[u][:, :, lo:hi].rearrange("p j (c i) -> p c j i", i=4),
            )

        def regroup_first(copy, half, lo, hi):
            copy(
                out=x_grouped[0][:, 256 * half + lo : 256 * half + hi, :].rearrange("p (c i) j -> p c j i", i=4),
                in_=(x_raw_a0, x_raw_a1)[half][:, :, lo:hi].rearrange("p j (c i) -> p c j i", i=4),
            )

        def quantise_x(u):
            nc.vector.quantize_mx(
                out=x_codes[u][:].bitcast(E4M3X4),
                scales=x_scales[u][:],
                in_=x_grouped[u][:].rearrange("p w j -> p (w j)"),
            )

        def regroup_g(copy, i):
            if i < 4:
                src, t0 = g_raw_first[:, :, :], i
            else:
                c = (i - 4) // 2
                src, t0 = g_raw_rest[:, :, c * 512 : (c + 1) * 512], 2 * ((i - 4) % 2)
            copy(
                out=g_grouped[i][:],
                in_=src.rearrange("p j (q t) -> p t q j", t=ROWS)[:, t0 : t0 + g_width[i], :, :],
            )

        def quantise_g(i):
            nc.vector.quantize_mx(
                out=g_codes[i][:].rearrange("p t q -> p (t q)").bitcast(E5M2X4),
                scales=g_scales[i][:].rearrange("p t q -> p (t q)"),
                in_=g_grouped[i][:].rearrange("p t q j -> p (t q j)"),
            )

        def one_pass(i, t, u):
            acc = psum.tile([P, N_TILE], F32)
            nc.tensor.matmul_mx(
                out=acc[:],
                lhsT=g_codes[i][:, t, :].bitcast(E5M2X4),
                lhsT_scale=g_scales[i][:, t, :],
                rhs=x_codes[u][:].bitcast(E4M3X4),
                rhs_scale=x_scales[u][:],
                start=True,
                stop=True,
            )
            return acc

        def store(c, t0, t1, n0, n1):
            nc.sync.dma_start(out=out_rows[c, :, t0:t1, n0:n1], in_=stage[:, c, t0:t1, n0:n1])

        regroup_first(vcopy, 0, 0, 256)
        regroup_first(vcopy, 1, 0, 192)
        regroup_first(scopy, 1, 192, 256)
        quantise_x(0)
        regroup_g(vcopy, 0)
        regroup_g(scopy, 1)
        regroup_g(scopy, 2)
        regroup_g(vcopy, 3)
        quantise_g(0)
        acc_a = [one_pass(0, 0, 0)]
        quantise_g(1)
        acc_a.append(one_pass(1, 0, 0))
        regroup_x(vcopy, 1, 0, 256)
        quantise_g(2)
        acc_a.append(one_pass(2, 0, 0))
        regroup_x(vcopy, 1, 256, 512)
        quantise_g(3)
        acc_a.append(one_pass(3, 0, 0))
        for t in range(4):
            scopy(out=stage[:, 0, t, 0:512], in_=acc_a[t][:])
            if t % 2 == 1:
                store(0, t - 1, t + 1, 0, 512)
        quantise_x(1)
        acc_b = [one_pass(t, 0, 1) for t in range(4)]
        regroup_x(vcopy, 2, 0, 512)
        regroup_x(scopy, 3, 448, 512)
        regroup_x(vcopy, 3, 0, 448)
        for t in range(4):
            scopy(out=stage[:, 0, t, 512:1024], in_=acc_b[t][:])
            if t % 2 == 1:
                store(0, t - 1, t + 1, 512, 1024)
        quantise_x(2)
        quantise_x(3)
        acc_c = [one_pass(0, 0, 2), one_pass(1, 0, 2)]
        acc_d = [one_pass(0, 0, 3), one_pass(1, 0, 3)]
        acc_c.extend([one_pass(2, 0, 2), one_pass(3, 0, 2)])
        acc_d.extend([one_pass(2, 0, 3), one_pass(3, 0, 3)])
        acc_cd = [(acc_c[t], acc_d[t]) for t in range(4)]
        regroup_g(vcopy, 4)
        for t in range(4):
            scopy(out=stage[:, 0, t, 1024:1536], in_=acc_cd[t][0][:])
            vcopy(out=stage[:, 0, t, 1536:2048], in_=acc_cd[t][1][:])
            if t < 2:
                store(0, t, t + 1, 1024, 2048)
            if t == 3:
                store(0, 2, 4, 1024, 2048)
            if t == 0:
                quantise_g(4)

        for i in range(4, 10):
            c, h = 1 + (i - 4) // 2, (i - 4) % 2
            banks = [(t, s, one_pass(i, t, s)) for t in range(2) for s in range(4)]
            if i + 1 < 10:
                regroup_g(vcopy, i + 1)
            for n, (t, s, acc) in enumerate(banks):
                copy = vcopy if n in (1, 4, 7) else scopy
                copy(out=stage[:, c, 2 * h + t, s * N_TILE : (s + 1) * N_TILE], in_=acc[:])
                if n == 1 and i + 1 < 10:
                    quantise_g(i + 1)
                if i == 4 and s == 3:
                    store(c, t, t + 1, 0, D_IN)
            if i == 5:
                store(c, 2, 4, 0, D_IN)
            if i > 5 and h == 1:
                store(c, 0, 4, 0, D_IN)
